import numpy as np
import ml_dtypes


def mxq(x, axis, fmt="e4m3"):
    dtype, down = {"e4m3": (ml_dtypes.float8_e4m3fn, 7), "e5m2": (ml_dtypes.float8_e5m2, 14)}[fmt]
    v = np.moveaxis(np.asarray(x, np.float32).astype(ml_dtypes.bfloat16).astype(np.float64), axis, -1)
    blocks = v.reshape(v.shape[:-1] + (-1, 32))
    amax = np.abs(blocks).max(-1, keepdims=True)
    byte = np.maximum(np.where(amax > 0, np.frexp(amax)[1] - 1 + 127, 0) - down, 1)
    scale = np.exp2(byte - 127.0)
    codes = (blocks / scale).astype(np.float32).astype(dtype).astype(np.float64)
    return np.moveaxis((codes * scale).reshape(v.shape), -1, axis)


WIDE = False


def mx_kscale(k):
    if not WIDE:
        return np.ones(k)
    levels = np.array([10, -10, 5, -5, 0])
    a = np.random.permutation(np.resize(levels, k // 512 * 4)).reshape(k // 512, 4)
    idx = np.arange(k)
    return np.exp2(a[idx // 512, idx % 128 // 32])


BF16 = ml_dtypes.bfloat16


def bf(x):
    return np.asarray(x, np.float32).astype(BF16)


def f64(x):
    return np.asarray(x).astype(np.float64)


B, L, H, G, DEPTH = 64, 64, 1024, 256, 3
EPS = 1e-5


def layernorm(v, g, b):
    mu = v.mean(-1, keepdims=True)
    var = np.square(v - mu).mean(-1, keepdims=True)
    return (v - mu) / np.sqrt(var + EPS) * g + b


def setup_inputs():
    s, t = mx_kscale(H), mx_kscale(H)
    return {"x_nodes": bf(np.random.standard_normal((B, L, H)) * s),
            "w1": bf(np.random.standard_normal((H, H)) / np.sqrt(H) / s[:, None]),
            "b1": bf(np.random.standard_normal(H) * 0.3),
            "gamma": bf((1.0 + 0.1 * np.random.standard_normal(H)) * t),
            "beta": bf(0.2 * np.random.standard_normal(H) * t),
            "w2": bf(np.random.standard_normal((H, G)) / np.sqrt(H) / t[:, None]),
            "b2": bf(np.random.standard_normal(G) * 0.3)}


def reference(x_nodes, w1, b1, gamma, beta, w2, b2):
    h = (mxq(f64(x_nodes), 2, "e4m3") @ mxq(f64(w1), 0, "e4m3")) + f64(b1)
    r = np.maximum(layernorm(h, f64(gamma), f64(beta)), 0.0)
    x1 = (mxq(r, 2, "e4m3") @ mxq(f64(w2), 0, "e4m3")) + f64(b2)
    x2 = np.broadcast_to(x1.max(axis=1, keepdims=True), x1.shape)
    return np.concatenate([x1, x2], axis=2)

@@ -1,0 +1,306 @@
+from contextlib import ExitStack
+
+import concourse.mybir as mybir
+from concourse.masks import make_identity
+
+F32 = mybir.dt.float32
+BF16 = mybir.dt.bfloat16
+U32 = mybir.dt.uint32
+U8 = mybir.dt.uint8
+FP8X4 = mybir.dt.float8_e4m3fn_x4
+ALU = mybir.AluOpType
+ACT = mybir.ActivationFunctionType
+AXIS = mybir.AxisListType
+
+P = 128
+PACK = 4
+K_PASS = P * PACK
+BANK = 512
+
+TOKENS = 64 * 64
+NODES = 64
+HIDDEN = 1024
+FEATURES = 256
+PASSES = HIDDEN // K_PASS
+SLICES = HIDDEN // P
+GROUP = 4
+GROUP_TOKENS = GROUP * P
+N_GROUPS = TOKENS // GROUP_TOKENS
+GROUP_LINES = GROUP_TOKENS // NODES
+COPIES = P // GROUP_LINES
+EPS = 1e-5
+
+FLOPS = 2 * TOKENS * HIDDEN * (HIDDEN + FEATURES)
+
+
+def regroup(nc, grouped, planes):
+    nc.vector.tensor_copy(
+        out=grouped.rearrange("p (n i) t -> p n t i", i=4),
+        in_=planes.rearrange("p t (n i) -> p n t i", i=4),
+    )
+
+
+def tile_sub_graph_pa_t_kernel(tc, x_nodes, w1, b1, gamma, beta, w2, b2, out):
+    nc = tc.nc
+    x_rows = x_nodes.flatten_outer_dims()
+    out_rows = out.flatten_outer_dims()
+
+    with ExitStack() as ctx:
+        consts = ctx.enter_context(tc.tile_pool(name="consts", bufs=1))
+        stage = ctx.enter_context(tc.tile_pool(name="stage", bufs=2))
+        psum = ctx.enter_context(tc.psum_pool(name="psum", bufs=1))
+
+        w1_planes = consts.tile([P, PASSES * PACK, HIDDEN], BF16)
+        w1_quarters = w1.rearrange("(a q e) n -> a q e n", a=4, q=P, e=2)
+
+        def load_w1_quarter(a):
+            nc.sync.dma_start(out=w1_planes[:, 2 * a : 2 * a + 2, :], in_=w1_quarters[a])
+
+        def load_x_group(group):
+            x_sb = stage.tile([P, GROUP, HIDDEN], BF16, tag="x_sb", bufs=4)
+            rows = x_rows[group * GROUP_TOKENS : (group + 1) * GROUP_TOKENS, :]
+            nc.sync.dma_start(out=x_sb[:], in_=rows.rearrange("(g p) k -> p g k", p=P))
+            return x_sb
+
+        load_w1_quarter(0)
+        load_w1_quarter(1)
+        x_groups = [load_x_group(0)]
+        load_w1_quarter(2)
+        load_w1_quarter(3)
+
+        b1_all = consts.tile([P, HIDDEN], BF16)
+        nc.sync.dma_start(out=b1_all[:], in_=b1.partition_broadcast(P))
+        b2_all = consts.tile([P, FEATURES], BF16)
+        nc.sync.dma_start(out=b2_all[:], in_=b2.partition_broadcast(P))
+
+        affine_rows = consts.tile([P, P], BF16)
+        nc.vector.memset(affine_rows[:], 0.0)
+        nc.sync.dma_start(
+            out=affine_rows[0:SLICES, :], in_=gamma.rearrange("(s p) -> s p", p=P)
+        )
+        nc.sync.dma_start(
+            out=affine_rows[SLICES : 2 * SLICES, :], in_=beta.rearrange("(s p) -> s p", p=P)
+        )
+
+        w2_planes = consts.tile([P, PASSES * PACK, FEATURES], BF16)
+        nc.sync.dma_start(
+            out=w2_planes[:], in_=w2.rearrange("(s p) n -> p s n", p=P)
+        )
+
+        ident = consts.tile([P, P], F32)
+        make_identity(nc, ident[:])
+        eps = consts.tile([P, 1], F32)
+        nc.vector.memset(eps[:], EPS)
+
+        affine_f32 = consts.tile([P, P], F32)
+        nc.vector.tensor_copy(out=affine_f32[:], in_=affine_rows[:])
+        affine_ps = psum.tile([P, P], F32, tag="pooled")
+        nc.tensor.transpose(out=affine_ps[:], in_=affine_f32[:], identity=ident[:])
+        affine_cols = consts.tile([P, 2 * SLICES], F32)
+        nc.vector.tensor_copy(out=affine_cols[:], in_=affine_ps[:, 0 : 2 * SLICES])
+
+        w1_codes = consts.tile([P, PASSES, HIDDEN], U32, align_bytes=64)
+        w1_scales = consts.tile([P, PASSES, HIDDEN], U8, align_bytes=64)
+        for half in range(HIDDEN // BANK):
+            cols = slice(half * BANK, (half + 1) * BANK)
+            for c in range(PASSES):
+                w1_grouped = stage.tile([P, BANK, PACK], BF16, tag="w1_grouped", align_bytes=64)
+                regroup(nc, w1_grouped[:], w1_planes[:, PACK * c : PACK * (c + 1), cols])
+                nc.vector.quantize_mx(
+                    out=w1_codes[:, c, cols].bitcast(FP8X4),
+                    scales=w1_scales[:, c, cols],
+                    in_=w1_grouped[:].rearrange("p n t -> p (n t)"),
+                )
+
+        w2_codes = consts.tile([P, PASSES, FEATURES], U32, align_bytes=64)
+        w2_scales = consts.tile([P, PASSES, FEATURES], U8, align_bytes=64)
+        for c in range(PASSES):
+            w2_grouped = stage.tile([P, FEATURES, PACK], BF16, tag="w2_grouped", align_bytes=64)
+            regroup(nc, w2_grouped[:], w2_planes[:, PACK * c : PACK * (c + 1), :])
+            nc.vector.quantize_mx(
+                out=w2_codes[:, c, :].bitcast(FP8X4),
+                scales=w2_scales[:, c, :],
+                in_=w2_grouped[:].rearrange("p n t -> p (n t)"),
+            )
+
+        def quantise_x_tile(x_sb, g):
+            words = x_sb[:, g, :].bitcast(F32)
+            xT_ps = psum.tile([P, PASSES, 2, P], F32, tag="xT", bufs=2)
+            for c in range(PASSES):
+                for u in range(2):
+                    a = 2 * c + u
+                    nc.tensor.transpose(
+                        out=xT_ps[:, c, u, :], in_=words[:, a * P : (a + 1) * P], identity=ident[:]
+                    )
+            x_grouped = stage.tile([P, PASSES, P, 2], F32, tag="x_grouped", bufs=3, align_bytes=64)
+            nc.scalar.copy(out=x_grouped[:], in_=xT_ps[:].rearrange("q c u r -> q c r u"))
+            x_codes = stage.tile([P, PASSES, P], U32, tag="x_codes", bufs=3, align_bytes=64)
+            x_scales = stage.tile([P, PASSES, P], U8, tag="x_scales", bufs=3, align_bytes=64)
+            nc.vector.quantize_mx(
+                out=x_codes[:].rearrange("q c r -> q (c r)").bitcast(FP8X4),
+                scales=x_scales[:].rearrange("q c r -> q (c r)"),
+                in_=x_grouped[:].rearrange("q c r u -> q (c r u)").bitcast(BF16),
+            )
+            return x_codes, x_scales
+
+        def first_layer_and_norm(x_codes, x_scales):
+            normed = stage.tile([P, HIDDEN], F32, tag="normed", bufs=10)
+            sums = stage.tile([P, HIDDEN // BANK], F32, tag="sums", bufs=4)
+            for half in range(HIDDEN // BANK):
+                cols = slice(half * BANK, (half + 1) * BANK)
+                h_ps = psum.tile([P, BANK], F32, tag="h", bufs=2)
+                for c in range(PASSES):
+                    nc.tensor.matmul_mx(
+                        out=h_ps[:],
+                        lhsT=x_codes[:, c, :].bitcast(FP8X4),
+                        lhsT_scale=x_scales[:, c, :],
+                        rhs=w1_codes[:, c, cols].bitcast(FP8X4),
+                        rhs_scale=w1_scales[:, c, cols],
+                        start=(c == 0),
+                        stop=(c == PASSES - 1),
+                    )
+                nc.vector.scalar_tensor_tensor(
+                    out=normed[:, cols],
+                    in0=h_ps[:],
+                    scalar=1.0,
+                    in1=b1_all[:, cols],
+                    op0=ALU.mult,
+                    op1=ALU.add,
+                    accum_out=sums[:, half : half + 1],
+                )
+            minus_mean = stage.tile([P, 1], F32, tag="minus_mean", bufs=4)
+            nc.vector.tensor_scalar(
+                out=minus_mean[:],
+                in0=sums[:, 0:1],
+                scalar1=sums[:, 1:2],
+                scalar2=-1.0 / HIDDEN,
+                op0=ALU.add,
+                op1=ALU.mult,
+            )
+            squares = stage.tile([P, HIDDEN], BF16, tag="squares", bufs=2)
+            sum_sq = stage.tile([P, 1], F32, tag="sum_sq", bufs=4)
+            nc.scalar.activation(
+                out=squares[:],
+                in_=normed[:],
+                func=ACT.Square,
+                bias=minus_mean[:, 0:1],
+                scale=1.0,
+                accum_out=sum_sq[:, 0:1],
+            )
+            std = stage.tile([P, 1], F32, tag="std", bufs=4)
+            nc.scalar.activation(
+                out=std[:], in_=sum_sq[:], func=ACT.Sqrt, bias=eps[:, 0:1], scale=1.0 / HIDDEN
+            )
+            inv_std = stage.tile([P, 1], F32, tag="inv_std", bufs=4)
+            nc.vector.reciprocal(out=inv_std[:], in_=std[:])
+            nc.vector.tensor_scalar(
+                out=normed[:],
+                in0=normed[:],
+                scalar1=minus_mean[:, 0:1],
+                scalar2=inv_std[:, 0:1],
+                op0=ALU.add,
+                op1=ALU.mult,
+            )
+            return normed
+
+        def quantise_r_group(normed_tiles):
+            r_planes = stage.tile([P, SLICES, GROUP_TOKENS], BF16, tag="r_planes", bufs=2)
+            r_codes = stage.tile([P, PASSES, GROUP_TOKENS], U32, tag="r_codes", bufs=2, align_bytes=64)
+            r_scales = stage.tile([P, PASSES, GROUP_TOKENS], U8, tag="r_scales", bufs=2, align_bytes=64)
+            for c in range(PASSES):
+                for t in range(PACK):
+                    s = PACK * c + t
+                    normedT_ps = psum.tile([P, GROUP_TOKENS], F32, tag="normedT", bufs=2)
+                    for g in range(GROUP):
+                        nc.tensor.transpose(
+                            out=normedT_ps[:, g * P : (g + 1) * P],
+                            in_=normed_tiles[g][:, s * P : (s + 1) * P],
+                            identity=ident[:],
+                        )
+                    nc.scalar.activation(
+                        out=r_planes[:, s, :],
+                        in_=normedT_ps[:],
+                        func=ACT.Relu,
+                        bias=affine_cols[:, SLICES + s : SLICES + s + 1],
+                        scale=affine_cols[:, s : s + 1],
+                    )
+                r_grouped = stage.tile([P, GROUP_TOKENS, PACK], BF16, tag="r_grouped", bufs=2, align_bytes=64)
+                regroup(nc, r_grouped[:], r_planes[:, PACK * c : PACK * (c + 1), :])
+                nc.vector.quantize_mx(
+                    out=r_codes[:, c, :].bitcast(FP8X4),
+                    scales=r_scales[:, c, :],
+                    in_=r_grouped[:].rearrange("p n t -> p (n t)"),
+                )
+            return r_codes, r_scales
+
+        def second_layer_and_pool(group, r_codes, r_scales):
+            rows = slice(group * GROUP_TOKENS, (group + 1) * GROUP_TOKENS)
+            x1_sb = stage.tile([P, GROUP, FEATURES], F32, tag="x1_sb", bufs=2)
+            line_max = stage.tile([P, FEATURES // P, GROUP_LINES], F32, tag="line_max", bufs=2)
+            for pair in range(GROUP // 2):
+                x1_ps = psum.tile([P, 2, FEATURES], F32, tag="x1")
+                for j in range(2):
+                    tokens = slice((2 * pair + j) * P, (2 * pair + j + 1) * P)
+                    for c in range(PASSES):
+                        nc.tensor.matmul_mx(
+                            out=x1_ps[:, j, :],
+                            lhsT=r_codes[:, c, tokens].bitcast(FP8X4),
+                            lhsT_scale=r_scales[:, c, tokens],
+                            rhs=w2_codes[:, c, :].bitcast(FP8X4),
+                            rhs_scale=w2_scales[:, c, :],
+                            start=(c == 0),
+                            stop=(c == PASSES - 1),
+                        )
+                nc.vector.tensor_tensor(
+                    out=x1_sb[:, 2 * pair : 2 * pair + 2, :],
+                    in0=x1_ps[:],
+                    in1=b2_all[:].unsqueeze(1).to_broadcast([P, 2, FEATURES]),
+                    op=ALU.add,
+                )
+                x1T_ps = psum.tile([P, FEATURES // P, 2 * P], F32, tag="pooled")
+                for s in range(FEATURES // P):
+                    for j in range(2):
+                        nc.tensor.transpose(
+                            out=x1T_ps[:, s, j * P : (j + 1) * P],
+                            in_=x1_sb[:, 2 * pair + j, s * P : (s + 1) * P],
+                            identity=ident[:],
+                        )
+                lines = 2 * P // NODES
+                nc.vector.tensor_reduce(
+                    out=line_max[:, :, pair * lines : (pair + 1) * lines],
+                    in_=x1T_ps[:].rearrange("f s (b l) -> f s b l", l=NODES),
+                    axis=AXIS.X,
+                    op=ALU.max,
+                )
+            nc.sync.dma_start(
+                out=out_rows[rows, 0:FEATURES].rearrange("(g p) f -> p g f", p=P), in_=x1_sb[:]
+            )
+            repeated = stage.tile([P, FEATURES // P, GROUP_LINES, COPIES], F32, tag="repeated", bufs=2)
+            nc.vector.tensor_copy(
+                out=repeated[:],
+                in_=line_max[:].unsqueeze(3).to_broadcast([P, FEATURES // P, GROUP_LINES, COPIES]),
+            )
+            x2_ps = psum.tile([P, FEATURES], F32, tag="pooled")
+            for s in range(FEATURES // P):
+                nc.tensor.transpose(
+                    out=x2_ps[:, s * P : (s + 1) * P],
+                    in_=repeated[:, s, :, :].rearrange("f b i -> f (b i)"),
+                    identity=ident[:],
+                )
+            x2_sb = stage.tile([P, FEATURES], F32, tag="x2_sb", bufs=2)
+            nc.scalar.copy(out=x2_sb[:], in_=x2_ps[:])
+            nodes_each = NODES // COPIES
+            nc.sync.dma_start(
+                out=out_rows[rows, FEATURES : 2 * FEATURES].rearrange("(p m) f -> p m f", m=nodes_each),
+                in_=x2_sb[:].unsqueeze(1).to_broadcast([P, nodes_each, FEATURES]),
+            )
+
+        for group in range(N_GROUPS):
+            if group + 1 < N_GROUPS:
+                x_groups.append(load_x_group(group + 1))
+            normed_tiles = []
+            for g in range(GROUP):
+                x_codes, x_scales = quantise_x_tile(x_groups[group], g)
+                normed_tiles.append(first_layer_and_norm(x_codes, x_scales))
+            r_codes, r_scales = quantise_r_group(normed_tiles)
+            second_layer_and_pool(group, r_codes, r_scales)

@@ -33,8 +33,27 @@ EPS = 1e-5
 FLOPS = 2 * TOKENS * HIDDEN * (HIDDEN + FEATURES)
 
 
-def regroup(nc, grouped, planes):
-    nc.vector.tensor_copy(
+N_TILES = TOKENS // P
+HALVES = HIDDEN // BANK
+PAIR_LINES = 2 * P // NODES
+
+X_AHEAD = 8
+RELU_LAG = 6
+QUANT_LAG = 8
+LAYER2_LAG = 11
+POOL_LAG = LAYER2_LAG + 2
+STORE_LAG = POOL_LAG + 3
+N_STEPS = N_TILES - GROUP + STORE_LAG + 1
+
+
+def due(step, lag, period):
+    if step < lag or (step - lag) % period != 0:
+        return -1
+    return (step - lag) // period
+
+
+def regroup(copy, grouped, planes):
+    copy(
         out=grouped.rearrange("p (n i) t -> p n t i", i=4),
         in_=planes.rearrange("p t (n i) -> p n t i", i=4),
     )
@@ -49,82 +68,59 @@ def tile_sub_graph_pa_t_kernel(tc, x_nodes, w1, b1, gamma, beta, w2, b2, out):
         consts = ctx.enter_context(tc.tile_pool(name="consts", bufs=1))
         stage = ctx.enter_context(tc.tile_pool(name="stage", bufs=2))
         psum = ctx.enter_context(tc.psum_pool(name="psum", bufs=1))
+        ctx.enter_context(tc.manual_schedule())
+
+        x_tiles, x_words, x_quantised = {}, {}, {}
+        normed, minus_mean, std = {}, {}, {}
+        r_planes, r_grouped, r_quantised = {}, {}, {}
+        x1_tiles, line_max, repeated = {}, {}, {}
+
+        def load_x(i):
+            if i >= N_TILES:
+                return
+            x_sb = stage.tile([P, HIDDEN], BF16, tag="x_sb", bufs=X_AHEAD + 2)
+            nc.sync.dma_start(out=x_sb[:], in_=x_rows[i * P : (i + 1) * P, :])
+            x_tiles[i] = x_sb
 
         w1_planes = consts.tile([P, PASSES * PACK, HIDDEN], BF16)
         w1_quarters = w1.rearrange("(a q e) n -> a q e n", a=4, q=P, e=2)
 
-        def load_w1_quarter(a):
-            nc.sync.dma_start(out=w1_planes[:, 2 * a : 2 * a + 2, :], in_=w1_quarters[a])
-
-        def load_x_group(group):
-            x_sb = stage.tile([P, GROUP, HIDDEN], BF16, tag="x_sb", bufs=4)
-            rows = x_rows[group * GROUP_TOKENS : (group + 1) * GROUP_TOKENS, :]
-            nc.sync.dma_start(out=x_sb[:], in_=rows.rearrange("(g p) k -> p g k", p=P))
-            return x_sb
-
-        load_w1_quarter(0)
-        load_w1_quarter(1)
-        x_groups = [load_x_group(0)]
-        load_w1_quarter(2)
-        load_w1_quarter(3)
-
-        b1_all = consts.tile([P, HIDDEN], BF16)
-        nc.sync.dma_start(out=b1_all[:], in_=b1.partition_broadcast(P))
-        b2_all = consts.tile([P, FEATURES], BF16)
-        nc.sync.dma_start(out=b2_all[:], in_=b2.partition_broadcast(P))
+        def load_w1_half(half):
+            cols = slice(half * BANK, (half + 1) * BANK)
+            for a in range(4):
+                nc.sync.dma_start(
+                    out=w1_planes[:, 2 * a : 2 * a + 2, cols], in_=w1_quarters[a][:, :, cols]
+                )
 
         affine_rows = consts.tile([P, P], BF16)
         nc.vector.memset(affine_rows[:], 0.0)
-        nc.sync.dma_start(
-            out=affine_rows[0:SLICES, :], in_=gamma.rearrange("(s p) -> s p", p=P)
-        )
-        nc.sync.dma_start(
-            out=affine_rows[SLICES : 2 * SLICES, :], in_=beta.rearrange("(s p) -> s p", p=P)
-        )
-
-        w2_planes = consts.tile([P, PASSES * PACK, FEATURES], BF16)
-        nc.sync.dma_start(
-            out=w2_planes[:], in_=w2.rearrange("(s p) n -> p s n", p=P)
-        )
-
-        ident = consts.tile([P, P], F32)
-        make_identity(nc, ident[:])
         eps = consts.tile([P, 1], F32)
         nc.vector.memset(eps[:], EPS)
+        ident = consts.tile([P, P], F32)
+        make_identity(nc, ident[:])
 
-        affine_f32 = consts.tile([P, P], F32)
-        nc.vector.tensor_copy(out=affine_f32[:], in_=affine_rows[:])
-        affine_ps = psum.tile([P, P], F32, tag="pooled")
-        nc.tensor.transpose(out=affine_ps[:], in_=affine_f32[:], identity=ident[:])
-        affine_cols = consts.tile([P, 2 * SLICES], F32)
-        nc.vector.tensor_copy(out=affine_cols[:], in_=affine_ps[:, 0 : 2 * SLICES])
+        nc.scalar.dma_start(out=affine_rows[0:SLICES, :], in_=gamma.rearrange("(s p) -> s p", p=P))
+        nc.scalar.dma_start(
+            out=affine_rows[SLICES : 2 * SLICES, :], in_=beta.rearrange("(s p) -> s p", p=P)
+        )
+        b1_all = consts.tile([P, HIDDEN], BF16)
+        nc.scalar.dma_start(out=b1_all[:], in_=b1.partition_broadcast(P))
+        b2_all = consts.tile([P, FEATURES], BF16)
+        nc.scalar.dma_start(out=b2_all[:], in_=b2.partition_broadcast(P))
 
-        w1_codes = consts.tile([P, PASSES, HIDDEN], U32, align_bytes=64)
-        w1_scales = consts.tile([P, PASSES, HIDDEN], U8, align_bytes=64)
-        for half in range(HIDDEN // BANK):
-            cols = slice(half * BANK, (half + 1) * BANK)
-            for c in range(PASSES):
-                w1_grouped = stage.tile([P, BANK, PACK], BF16, tag="w1_grouped", align_bytes=64)
-                regroup(nc, w1_grouped[:], w1_planes[:, PACK * c : PACK * (c + 1), cols])
-                nc.vector.quantize_mx(
-                    out=w1_codes[:, c, cols].bitcast(FP8X4),
-                    scales=w1_scales[:, c, cols],
-                    in_=w1_grouped[:].rearrange("p n t -> p (n t)"),
-                )
+        load_x(0)
+        load_w1_half(0)
+        load_x(1)
+        load_w1_half(1)
+        w2_planes = consts.tile([P, PASSES * PACK, FEATURES], BF16)
+        nc.sync.dma_start(out=w2_planes[:], in_=w2.rearrange("(s p) n -> p s n", p=P))
+        for i in range(2, X_AHEAD):
+            load_x(i)
 
-        w2_codes = consts.tile([P, PASSES, FEATURES], U32, align_bytes=64)
-        w2_scales = consts.tile([P, PASSES, FEATURES], U8, align_bytes=64)
-        for c in range(PASSES):
-            w2_grouped = stage.tile([P, FEATURES, PACK], BF16, tag="w2_grouped", align_bytes=64)
-            regroup(nc, w2_grouped[:], w2_planes[:, PACK * c : PACK * (c + 1), :])
-            nc.vector.quantize_mx(
-                out=w2_codes[:, c, :].bitcast(FP8X4),
-                scales=w2_scales[:, c, :],
-                in_=w2_grouped[:].rearrange("p n t -> p (n t)"),
-            )
-
-        def quantise_x_tile(x_sb, g):
-            words = x_sb[:, g, :].bitcast(F32)
+        def transpose_x(i):
+            if i >= N_TILES:
+                return
+            words = x_tiles[i][:].bitcast(F32)
             xT_ps = psum.tile([P, PASSES, 2, P], F32, tag="xT", bufs=2)
             for c in range(PASSES):
                 for u in range(2):
@@ -134,19 +130,27 @@ def tile_sub_graph_pa_t_kernel(tc, x_nodes, w1, b1, gamma, beta, w2, b2, out):
                     )
             x_grouped = stage.tile([P, PASSES, P, 2], F32, tag="x_grouped", bufs=3, align_bytes=64)
             nc.scalar.copy(out=x_grouped[:], in_=xT_ps[:].rearrange("q c u r -> q c r u"))
+            x_words[i] = x_grouped
+
+        def quantise_x(i):
+            if i >= N_TILES:
+                return
             x_codes = stage.tile([P, PASSES, P], U32, tag="x_codes", bufs=3, align_bytes=64)
             x_scales = stage.tile([P, PASSES, P], U8, tag="x_scales", bufs=3, align_bytes=64)
             nc.vector.quantize_mx(
                 out=x_codes[:].rearrange("q c r -> q (c r)").bitcast(FP8X4),
                 scales=x_scales[:].rearrange("q c r -> q (c r)"),
-                in_=x_grouped[:].rearrange("q c r u -> q (c r u)").bitcast(BF16),
+                in_=x_words[i][:].rearrange("q c r u -> q (c r u)").bitcast(BF16),
             )
-            return x_codes, x_scales
+            x_quantised[i] = (x_codes, x_scales)
 
-        def first_layer_and_norm(x_codes, x_scales):
-            normed = stage.tile([P, HIDDEN], F32, tag="normed", bufs=10)
-            sums = stage.tile([P, HIDDEN // BANK], F32, tag="sums", bufs=4)
-            for half in range(HIDDEN // BANK):
+        def first_layer(i):
+            if i >= N_TILES:
+                return
+            x_codes, x_scales = x_quantised[i]
+            biased = stage.tile([P, HIDDEN], F32, tag="normed", bufs=12)
+            sums = stage.tile([P, HALVES], F32, tag="sums", bufs=3)
+            for half in range(HALVES):
                 cols = slice(half * BANK, (half + 1) * BANK)
                 h_ps = psum.tile([P, BANK], F32, tag="h", bufs=2)
                 for c in range(PASSES):
@@ -160,7 +164,7 @@ def tile_sub_graph_pa_t_kernel(tc, x_nodes, w1, b1, gamma, beta, w2, b2, out):
                         stop=(c == PASSES - 1),
                     )
                 nc.vector.scalar_tensor_tensor(
-                    out=normed[:, cols],
+                    out=biased[:, cols],
                     in0=h_ps[:],
                     scalar=1.0,
                     in1=b1_all[:, cols],
@@ -168,139 +172,230 @@ def tile_sub_graph_pa_t_kernel(tc, x_nodes, w1, b1, gamma, beta, w2, b2, out):
                     op1=ALU.add,
                     accum_out=sums[:, half : half + 1],
                 )
-            minus_mean = stage.tile([P, 1], F32, tag="minus_mean", bufs=4)
+            negated = stage.tile([P, 1], F32, tag="minus_mean", bufs=6)
             nc.vector.tensor_scalar(
-                out=minus_mean[:],
+                out=negated[:],
                 in0=sums[:, 0:1],
                 scalar1=sums[:, 1:2],
                 scalar2=-1.0 / HIDDEN,
                 op0=ALU.add,
                 op1=ALU.mult,
             )
+            normed[i] = biased
+            minus_mean[i] = negated
+
+        def deviation(i):
+            if not 0 <= i < N_TILES:
+                return
             squares = stage.tile([P, HIDDEN], BF16, tag="squares", bufs=2)
-            sum_sq = stage.tile([P, 1], F32, tag="sum_sq", bufs=4)
+            sum_sq = stage.tile([P, 1], F32, tag="sum_sq", bufs=3)
             nc.scalar.activation(
                 out=squares[:],
-                in_=normed[:],
+                in_=normed[i][:],
                 func=ACT.Square,
-                bias=minus_mean[:, 0:1],
+                bias=minus_mean[i][:, 0:1],
                 scale=1.0,
                 accum_out=sum_sq[:, 0:1],
             )
-            std = stage.tile([P, 1], F32, tag="std", bufs=4)
+            root = stage.tile([P, 1], F32, tag="std", bufs=3)
             nc.scalar.activation(
-                out=std[:], in_=sum_sq[:], func=ACT.Sqrt, bias=eps[:, 0:1], scale=1.0 / HIDDEN
+                out=root[:], in_=sum_sq[:], func=ACT.Sqrt, bias=eps[:, 0:1], scale=1.0 / HIDDEN
             )
-            inv_std = stage.tile([P, 1], F32, tag="inv_std", bufs=4)
-            nc.vector.reciprocal(out=inv_std[:], in_=std[:])
+            std[i] = root
+
+        def normalise(i):
+            if not 0 <= i < N_TILES:
+                return
+            inverse = stage.tile([P, 1], F32, tag="inv_std", bufs=3)
+            nc.vector.reciprocal(out=inverse[:], in_=std[i][:])
             nc.vector.tensor_scalar(
-                out=normed[:],
-                in0=normed[:],
-                scalar1=minus_mean[:, 0:1],
-                scalar2=inv_std[:, 0:1],
+                out=normed[i][:],
+                in0=normed[i][:],
+                scalar1=minus_mean[i][:, 0:1],
+                scalar2=inverse[:, 0:1],
                 op0=ALU.add,
                 op1=ALU.mult,
             )
-            return normed
 
-        def quantise_r_group(normed_tiles):
-            r_planes = stage.tile([P, SLICES, GROUP_TOKENS], BF16, tag="r_planes", bufs=2)
-            r_codes = stage.tile([P, PASSES, GROUP_TOKENS], U32, tag="r_codes", bufs=2, align_bytes=64)
-            r_scales = stage.tile([P, PASSES, GROUP_TOKENS], U8, tag="r_scales", bufs=2, align_bytes=64)
-            for c in range(PASSES):
-                for t in range(PACK):
-                    s = PACK * c + t
-                    normedT_ps = psum.tile([P, GROUP_TOKENS], F32, tag="normedT", bufs=2)
-                    for g in range(GROUP):
-                        nc.tensor.transpose(
-                            out=normedT_ps[:, g * P : (g + 1) * P],
-                            in_=normed_tiles[g][:, s * P : (s + 1) * P],
-                            identity=ident[:],
-                        )
-                    nc.scalar.activation(
-                        out=r_planes[:, s, :],
-                        in_=normedT_ps[:],
-                        func=ACT.Relu,
-                        bias=affine_cols[:, SLICES + s : SLICES + s + 1],
-                        scale=affine_cols[:, s : s + 1],
+        def relu_slice(index):
+            if not 0 <= index < N_GROUPS * SLICES:
+                return
+            group, s = divmod(index, SLICES)
+            if s == 0:
+                planes = stage.tile([P, SLICES, GROUP_TOKENS], BF16, tag="r_planes", bufs=2)
+                r_planes[group] = planes
+            normedT_ps = psum.tile([P, GROUP_TOKENS], F32, tag="normedT", bufs=2)
+            for g in range(GROUP):
+                nc.tensor.transpose(
+                    out=normedT_ps[:, g * P : (g + 1) * P],
+                    in_=normed[group * GROUP + g][:, s * P : (s + 1) * P],
+                    identity=ident[:],
+                )
+            nc.scalar.activation(
+                out=r_planes[group][:, s, :],
+                in_=normedT_ps[:],
+                func=ACT.Relu,
+                bias=affine_cols[:, SLICES + s : SLICES + s + 1],
+                scale=affine_cols[:, s : s + 1],
+            )
+
+        def regroup_r(index):
+            if not 0 <= index < N_GROUPS * PASSES:
+                return
+            group, c = divmod(index, PASSES)
+            grouped = stage.tile([P, GROUP_TOKENS, PACK], BF16, tag="r_grouped", bufs=2, align_bytes=64)
+            regroup(nc.vector.tensor_copy, grouped[:], r_planes[group][:, PACK * c : PACK * (c + 1), :])
+            r_grouped[index] = grouped
+
+        def quantise_r(index):
+            if not 0 <= index < N_GROUPS * PASSES:
+                return
+            group, c = divmod(index, PASSES)
+            if c == 0:
+                codes = stage.tile([P, PASSES, GROUP_TOKENS], U32, tag="r_codes", bufs=2, align_bytes=64)
+                scales = stage.tile([P, PASSES, GROUP_TOKENS], U8, tag="r_scales", bufs=2, align_bytes=64)
+                r_quantised[group] = (codes, scales)
+            r_codes, r_scales = r_quantised[group]
+            nc.vector.quantize_mx(
+                out=r_codes[:, c, :].bitcast(FP8X4),
+                scales=r_scales[:, c, :],
+                in_=r_grouped[index][:].rearrange("p n t -> p (n t)"),
+            )
+
+        def second_layer(index):
+            if not 0 <= index < N_TILES // 2:
+                return
+            group, pair = divmod(index, GROUP // 2)
+            if pair == 0:
+                x1_sb = stage.tile([P, GROUP, FEATURES], F32, tag="x1_sb", bufs=3)
+                x1_tiles[group] = x1_sb
+            r_codes, r_scales = r_quantised[group]
+            x1_ps = psum.tile([P, 2, FEATURES], F32, tag="x1")
+            for j in range(2):
+                tokens = slice((2 * pair + j) * P, (2 * pair + j + 1) * P)
+                for c in range(PASSES):
+                    nc.tensor.matmul_mx(
+                        out=x1_ps[:, j, :],
+                        lhsT=r_codes[:, c, tokens].bitcast(FP8X4),
+                        lhsT_scale=r_scales[:, c, tokens],
+                        rhs=w2_codes[:, c, :].bitcast(FP8X4),
+                        rhs_scale=w2_scales[:, c, :],
+                        start=(c == 0),
+                        stop=(c == PASSES - 1),
                     )
-                r_grouped = stage.tile([P, GROUP_TOKENS, PACK], BF16, tag="r_grouped", bufs=2, align_bytes=64)
-                regroup(nc, r_grouped[:], r_planes[:, PACK * c : PACK * (c + 1), :])
-                nc.vector.quantize_mx(
-                    out=r_codes[:, c, :].bitcast(FP8X4),
-                    scales=r_scales[:, c, :],
-                    in_=r_grouped[:].rearrange("p n t -> p (n t)"),
+            nc.vector.tensor_tensor(
+                out=x1_tiles[group][:, 2 * pair : 2 * pair + 2, :],
+                in0=x1_ps[:],
+                in1=b2_all[:].unsqueeze(1).to_broadcast([P, 2, FEATURES]),
+                op=ALU.add,
+            )
+            if pair == GROUP // 2 - 1:
+                rows = slice(group * GROUP_TOKENS, (group + 1) * GROUP_TOKENS)
+                nc.sync.dma_start(
+                    out=out_rows[rows, 0:FEATURES].rearrange("(g p) f -> p g f", p=P),
+                    in_=x1_tiles[group][:],
                 )
-            return r_codes, r_scales
 
-        def second_layer_and_pool(group, r_codes, r_scales):
-            rows = slice(group * GROUP_TOKENS, (group + 1) * GROUP_TOKENS)
-            x1_sb = stage.tile([P, GROUP, FEATURES], F32, tag="x1_sb", bufs=2)
-            line_max = stage.tile([P, FEATURES // P, GROUP_LINES], F32, tag="line_max", bufs=2)
-            for pair in range(GROUP // 2):
-                x1_ps = psum.tile([P, 2, FEATURES], F32, tag="x1")
+        def pool_pair(index):
+            if not 0 <= index < N_TILES // 2:
+                return
+            group, pair = divmod(index, GROUP // 2)
+            if pair == 0:
+                maxima = stage.tile([P, FEATURES // P, GROUP_LINES], F32, tag="line_max", bufs=2)
+                line_max[group] = maxima
+            x1T_ps = psum.tile([P, FEATURES // P, 2 * P], F32, tag="pooled")
+            for s in range(FEATURES // P):
                 for j in range(2):
-                    tokens = slice((2 * pair + j) * P, (2 * pair + j + 1) * P)
-                    for c in range(PASSES):
-                        nc.tensor.matmul_mx(
-                            out=x1_ps[:, j, :],
-                            lhsT=r_codes[:, c, tokens].bitcast(FP8X4),
-                            lhsT_scale=r_scales[:, c, tokens],
-                            rhs=w2_codes[:, c, :].bitcast(FP8X4),
-                            rhs_scale=w2_scales[:, c, :],
-                            start=(c == 0),
-                            stop=(c == PASSES - 1),
-                        )
-                nc.vector.tensor_tensor(
-                    out=x1_sb[:, 2 * pair : 2 * pair + 2, :],
-                    in0=x1_ps[:],
-                    in1=b2_all[:].unsqueeze(1).to_broadcast([P, 2, FEATURES]),
-                    op=ALU.add,
-                )
-                x1T_ps = psum.tile([P, FEATURES // P, 2 * P], F32, tag="pooled")
-                for s in range(FEATURES // P):
-                    for j in range(2):
-                        nc.tensor.transpose(
-                            out=x1T_ps[:, s, j * P : (j + 1) * P],
-                            in_=x1_sb[:, 2 * pair + j, s * P : (s + 1) * P],
-                            identity=ident[:],
-                        )
-                lines = 2 * P // NODES
-                nc.vector.tensor_reduce(
-                    out=line_max[:, :, pair * lines : (pair + 1) * lines],
-                    in_=x1T_ps[:].rearrange("f s (b l) -> f s b l", l=NODES),
-                    axis=AXIS.X,
-                    op=ALU.max,
-                )
-            nc.sync.dma_start(
-                out=out_rows[rows, 0:FEATURES].rearrange("(g p) f -> p g f", p=P), in_=x1_sb[:]
+                    nc.tensor.transpose(
+                        out=x1T_ps[:, s, j * P : (j + 1) * P],
+                        in_=x1_tiles[group][:, 2 * pair + j, s * P : (s + 1) * P],
+                        identity=ident[:],
+                    )
+            nc.vector.tensor_reduce(
+                out=line_max[group][:, :, pair * PAIR_LINES : (pair + 1) * PAIR_LINES],
+                in_=x1T_ps[:].rearrange("f s (b l) -> f s b l", l=NODES),
+                axis=AXIS.X,
+                op=ALU.max,
             )
-            repeated = stage.tile([P, FEATURES // P, GROUP_LINES, COPIES], F32, tag="repeated", bufs=2)
-            nc.vector.tensor_copy(
-                out=repeated[:],
-                in_=line_max[:].unsqueeze(3).to_broadcast([P, FEATURES // P, GROUP_LINES, COPIES]),
-            )
+            if pair == GROUP // 2 - 1:
+                copies = stage.tile([P, FEATURES // P, GROUP_LINES, COPIES], F32, tag="repeated", bufs=2)
+                nc.vector.tensor_copy(
+                    out=copies[:],
+                    in_=line_max[group][:].unsqueeze(3).to_broadcast([P, FEATURES // P, GROUP_LINES, COPIES]),
+                )
+                repeated[group] = copies
+
+        def store_pooled(group):
+            if not 0 <= group < N_GROUPS:
+                return
             x2_ps = psum.tile([P, FEATURES], F32, tag="pooled")
             for s in range(FEATURES // P):
                 nc.tensor.transpose(
                     out=x2_ps[:, s * P : (s + 1) * P],
-                    in_=repeated[:, s, :, :].rearrange("f b i -> f (b i)"),
+                    in_=repeated[group][:, s, :, :].rearrange("f b i -> f (b i)"),
                     identity=ident[:],
                 )
             x2_sb = stage.tile([P, FEATURES], F32, tag="x2_sb", bufs=2)
             nc.scalar.copy(out=x2_sb[:], in_=x2_ps[:])
+            rows = slice(group * GROUP_TOKENS, (group + 1) * GROUP_TOKENS)
             nodes_each = NODES // COPIES
             nc.sync.dma_start(
                 out=out_rows[rows, FEATURES : 2 * FEATURES].rearrange("(p m) f -> p m f", m=nodes_each),
                 in_=x2_sb[:].unsqueeze(1).to_broadcast([P, nodes_each, FEATURES]),
             )
 
-        for group in range(N_GROUPS):
-            if group + 1 < N_GROUPS:
-                x_groups.append(load_x_group(group + 1))
-            normed_tiles = []
-            for g in range(GROUP):
-                x_codes, x_scales = quantise_x_tile(x_groups[group], g)
-                normed_tiles.append(first_layer_and_norm(x_codes, x_scales))
-            r_codes, r_scales = quantise_r_group(normed_tiles)
-            second_layer_and_pool(group, r_codes, r_scales)
+        transpose_x(0)
+
+        w1_codes = consts.tile([P, PASSES, HIDDEN], U32, align_bytes=64)
+        w1_scales = consts.tile([P, PASSES, HIDDEN], U8, align_bytes=64)
+
+        def quantise_w1_half(half):
+            cols = slice(half * BANK, (half + 1) * BANK)
+            grouped_passes = []
+            for c in range(PASSES):
+                w1_grouped = stage.tile([P, BANK, PACK], BF16, tag="w1_grouped", bufs=2, align_bytes=64)
+                regroup(nc.vector.tensor_copy, w1_grouped[:], w1_planes[:, PACK * c : PACK * (c + 1), cols])
+                grouped_passes.append(w1_grouped)
+            for c in range(PASSES):
+                nc.vector.quantize_mx(
+                    out=w1_codes[:, c, cols].bitcast(FP8X4),
+                    scales=w1_scales[:, c, cols],
+                    in_=grouped_passes[c][:].rearrange("p n t -> p (n t)"),
+                )
+
+        quantise_w1_half(0)
+        quantise_x(0)
+        affine_f32 = consts.tile([P, P], F32)
+        nc.vector.tensor_copy(out=affine_f32[:], in_=affine_rows[:])
+        affine_ps = psum.tile([P, P], F32, tag="pooled")
+        nc.tensor.transpose(out=affine_ps[:], in_=affine_f32[:], identity=ident[:])
+        quantise_w1_half(1)
+        affine_cols = consts.tile([P, 2 * SLICES], F32)
+        nc.vector.tensor_copy(out=affine_cols[:], in_=affine_ps[:, 0 : 2 * SLICES])
+
+        w2_grouped = consts.tile([P, PASSES, FEATURES, PACK], BF16, align_bytes=64)
+        for c in range(PASSES):
+            regroup(nc.scalar.copy, w2_grouped[:, c, :, :], w2_planes[:, PACK * c : PACK * (c + 1), :])
+        w2_codes = consts.tile([P, PASSES, FEATURES], U32, align_bytes=64)
+        w2_scales = consts.tile([P, PASSES, FEATURES], U8, align_bytes=64)
+
+        for step in range(N_STEPS):
+            load_x(step + X_AHEAD)
+            normalise(step - 2)
+            regroup_r(due(step, QUANT_LAG, 2))
+            transpose_x(step + 1)
+            relu_slice(2 * (step - RELU_LAG))
+            relu_slice(2 * (step - RELU_LAG) + 1)
+            pool_pair(due(step, POOL_LAG, 2))
+            store_pooled(due(step, STORE_LAG, GROUP))
+            deviation(step - 1)
+            quantise_x(step + 1)
+            first_layer(step)
+            second_layer(due(step, LAYER2_LAG, 2))
+            quantise_r(due(step, QUANT_LAG, 2))
+            if step == 0:
+                nc.vector.quantize_mx(
+                    out=w2_codes[:].rearrange("p c n -> p (c n)").bitcast(FP8X4),
+                    scales=w2_scales[:].rearrange("p c n -> p (c n)"),
+                    in_=w2_grouped[:].rearrange("p c n t -> p (c n t)"),
+                )

@@ -38,9 +38,9 @@ HALVES = HIDDEN // BANK
 PAIR_LINES = 2 * P // NODES
 
 X_AHEAD = 8
-RELU_LAG = 6
-QUANT_LAG = 8
-LAYER2_LAG = 11
+RELU_LAG = 7
+QUANT_LAG = 9
+LAYER2_LAG = 12
 POOL_LAG = LAYER2_LAG + 2
 STORE_LAG = POOL_LAG + 3
 N_STEPS = N_TILES - GROUP + STORE_LAG + 1
@@ -71,7 +71,7 @@ def tile_sub_graph_pa_t_kernel(tc, x_nodes, w1, b1, gamma, beta, w2, b2, out):
         ctx.enter_context(tc.manual_schedule())
 
         x_tiles, x_words, x_quantised = {}, {}, {}
-        normed, minus_mean, std = {}, {}, {}
+        normed, minus_mean, squared = {}, {}, {}
         r_planes, r_grouped, r_quantised = {}, {}, {}
         x1_tiles, line_max, repeated = {}, {}, {}
 
@@ -94,8 +94,8 @@ def tile_sub_graph_pa_t_kernel(tc, x_nodes, w1, b1, gamma, beta, w2, b2, out):
 
         affine_rows = consts.tile([P, P], BF16)
         nc.vector.memset(affine_rows[:], 0.0)
-        eps = consts.tile([P, 1], F32)
-        nc.vector.memset(eps[:], EPS)
+        minus_half = consts.tile([P, 1], F32)
+        nc.vector.memset(minus_half[:], -0.5)
         ident = consts.tile([P, P], F32)
         make_identity(nc, ident[:])
 
@@ -173,7 +173,7 @@ def tile_sub_graph_pa_t_kernel(tc, x_nodes, w1, b1, gamma, beta, w2, b2, out):
                     accum_out=sums[:, half : half + 1],
                 )
             negated = stage.tile([P, 1], F32, tag="minus_mean", bufs=6)
-            nc.vector.tensor_scalar(
+            nc.gpsimd.tensor_scalar(
                 out=negated[:],
                 in0=sums[:, 0:1],
                 scalar1=sums[:, 1:2],
@@ -188,7 +188,7 @@ def tile_sub_graph_pa_t_kernel(tc, x_nodes, w1, b1, gamma, beta, w2, b2, out):
             if not 0 <= i < N_TILES:
                 return
             squares = stage.tile([P, HIDDEN], BF16, tag="squares", bufs=2)
-            sum_sq = stage.tile([P, 1], F32, tag="sum_sq", bufs=3)
+            sum_sq = stage.tile([P, 1], F32, tag="sum_sq", bufs=4)
             nc.scalar.activation(
                 out=squares[:],
                 in_=normed[i][:],
@@ -197,25 +197,32 @@ def tile_sub_graph_pa_t_kernel(tc, x_nodes, w1, b1, gamma, beta, w2, b2, out):
                 scale=1.0,
                 accum_out=sum_sq[:, 0:1],
             )
-            root = stage.tile([P, 1], F32, tag="std", bufs=3)
-            nc.scalar.activation(
-                out=root[:], in_=sum_sq[:], func=ACT.Sqrt, bias=eps[:, 0:1], scale=1.0 / HIDDEN
-            )
-            std[i] = root
+            squared[i] = sum_sq
 
         def normalise(i):
             if not 0 <= i < N_TILES:
                 return
-            inverse = stage.tile([P, 1], F32, tag="inv_std", bufs=3)
-            nc.vector.reciprocal(out=inverse[:], in_=std[i][:])
-            nc.vector.tensor_scalar(
-                out=normed[i][:],
-                in0=normed[i][:],
-                scalar1=minus_mean[i][:, 0:1],
-                scalar2=inverse[:, 0:1],
-                op0=ALU.add,
-                op1=ALU.mult,
+            var_eps = stage.tile([P, 1], F32, tag="var_eps", bufs=3)
+            nc.gpsimd.tensor_scalar(
+                out=var_eps[:],
+                in0=squared[i][:],
+                scalar1=1.0 / HIDDEN,
+                scalar2=EPS,
+                op0=ALU.mult,
+                op1=ALU.add,
             )
+            inverse = stage.tile([P, 1], F32, tag="inv_std", bufs=3)
+            nc.gpsimd.tensor_tensor(out=inverse[:], in0=var_eps[:], in1=minus_half[:], op=ALU.pow)
+            for half in range(HALVES):
+                cols = slice(half * BANK, (half + 1) * BANK)
+                nc.gpsimd.tensor_scalar(
+                    out=normed[i][:, cols],
+                    in0=normed[i][:, cols],
+                    scalar1=minus_mean[i][:, 0:1],
+                    scalar2=inverse[:, 0:1],
+                    op0=ALU.add,
+                    op1=ALU.mult,
+                )
 
         def relu_slice(index):
             if not 0 <= index < N_GROUPS * SLICES:
@@ -345,6 +352,7 @@ def tile_sub_graph_pa_t_kernel(tc, x_nodes, w1, b1, gamma, beta, w2, b2, out):
             )
 
         transpose_x(0)
+        transpose_x(1)
 
         w1_codes = consts.tile([P, PASSES, HIDDEN], U32, align_bytes=64)
         w1_scales = consts.tile([P, PASSES, HIDDEN], U8, align_bytes=64)
@@ -383,16 +391,16 @@ def tile_sub_graph_pa_t_kernel(tc, x_nodes, w1, b1, gamma, beta, w2, b2, out):
             load_x(step + X_AHEAD)
             normalise(step - 2)
             regroup_r(due(step, QUANT_LAG, 2))
-            transpose_x(step + 1)
+            quantise_x(step + 1)
+            quantise_r(due(step, QUANT_LAG, 2))
+            transpose_x(step + 2)
             relu_slice(2 * (step - RELU_LAG))
             relu_slice(2 * (step - RELU_LAG) + 1)
             pool_pair(due(step, POOL_LAG, 2))
             store_pooled(due(step, STORE_LAG, GROUP))
             deviation(step - 1)
-            quantise_x(step + 1)
             first_layer(step)
             second_layer(due(step, LAYER2_LAG, 2))
-            quantise_r(due(step, QUANT_LAG, 2))
             if step == 0:
                 nc.vector.quantize_mx(
                     out=w2_codes[:].rearrange("p c n -> p (c n)").bitcast(FP8X4),

@@ -38,9 +38,9 @@ HALVES = HIDDEN // BANK
 PAIR_LINES = 2 * P // NODES
 
 X_AHEAD = 8
-RELU_LAG = 7
-QUANT_LAG = 9
-LAYER2_LAG = 12
+RELU_LAG = 6
+QUANT_LAG = 8
+LAYER2_LAG = 11
 POOL_LAG = LAYER2_LAG + 2
 STORE_LAG = POOL_LAG + 3
 N_STEPS = N_TILES - GROUP + STORE_LAG + 1
@@ -68,10 +68,9 @@ def tile_sub_graph_pa_t_kernel(tc, x_nodes, w1, b1, gamma, beta, w2, b2, out):
         consts = ctx.enter_context(tc.tile_pool(name="consts", bufs=1))
         stage = ctx.enter_context(tc.tile_pool(name="stage", bufs=2))
         psum = ctx.enter_context(tc.psum_pool(name="psum", bufs=1))
-        ctx.enter_context(tc.manual_schedule())
 
         x_tiles, x_words, x_quantised = {}, {}, {}
-        normed, minus_mean, squared = {}, {}, {}
+        normed, row_sums, minus_mean, inv_std = {}, {}, {}, {}
         r_planes, r_grouped, r_quantised = {}, {}, {}
         x1_tiles, line_max, repeated = {}, {}, {}
 
@@ -94,8 +93,8 @@ def tile_sub_graph_pa_t_kernel(tc, x_nodes, w1, b1, gamma, beta, w2, b2, out):
 
         affine_rows = consts.tile([P, P], BF16)
         nc.vector.memset(affine_rows[:], 0.0)
-        minus_half = consts.tile([P, 1], F32)
-        nc.vector.memset(minus_half[:], -0.5)
+        eps = consts.tile([P, 1], F32)
+        nc.vector.memset(eps[:], EPS)
         ident = consts.tile([P, P], F32)
         make_identity(nc, ident[:])
 
@@ -149,7 +148,7 @@ def tile_sub_graph_pa_t_kernel(tc, x_nodes, w1, b1, gamma, beta, w2, b2, out):
                 return
             x_codes, x_scales = x_quantised[i]
             biased = stage.tile([P, HIDDEN], F32, tag="normed", bufs=12)
-            sums = stage.tile([P, HALVES], F32, tag="sums", bufs=3)
+            sums = stage.tile([P, HALVES], F32, tag="sums", bufs=4)
             for half in range(HALVES):
                 cols = slice(half * BANK, (half + 1) * BANK)
                 h_ps = psum.tile([P, BANK], F32, tag="h", bufs=2)
@@ -172,23 +171,24 @@ def tile_sub_graph_pa_t_kernel(tc, x_nodes, w1, b1, gamma, beta, w2, b2, out):
                     op1=ALU.add,
                     accum_out=sums[:, half : half + 1],
                 )
-            negated = stage.tile([P, 1], F32, tag="minus_mean", bufs=6)
-            nc.gpsimd.tensor_scalar(
-                out=negated[:],
-                in0=sums[:, 0:1],
-                scalar1=sums[:, 1:2],
-                scalar2=-1.0 / HIDDEN,
-                op0=ALU.add,
-                op1=ALU.mult,
-            )
             normed[i] = biased
-            minus_mean[i] = negated
+            row_sums[i] = sums
 
         def deviation(i):
             if not 0 <= i < N_TILES:
                 return
+            scaled_sums = stage.tile([P, HALVES], F32, tag="scaled_sums", bufs=2)
+            negated = stage.tile([P, 1], F32, tag="minus_mean", bufs=6)
+            nc.scalar.activation(
+                out=scaled_sums[:],
+                in_=row_sums[i][:],
+                func=ACT.Identity,
+                scale=-1.0 / HIDDEN,
+                accum_out=negated[:, 0:1],
+            )
+            minus_mean[i] = negated
             squares = stage.tile([P, HIDDEN], BF16, tag="squares", bufs=2)
-            sum_sq = stage.tile([P, 1], F32, tag="sum_sq", bufs=4)
+            sum_sq = stage.tile([P, 1], F32, tag="sum_sq", bufs=3)
             nc.scalar.activation(
                 out=squares[:],
                 in_=normed[i][:],
@@ -197,32 +197,27 @@ def tile_sub_graph_pa_t_kernel(tc, x_nodes, w1, b1, gamma, beta, w2, b2, out):
                 scale=1.0,
                 accum_out=sum_sq[:, 0:1],
             )
-            squared[i] = sum_sq
+            inverse = stage.tile([P, 1], F32, tag="inv_std", bufs=4)
+            nc.scalar.activation(
+                out=inverse[:],
+                in_=sum_sq[:],
+                func=ACT.Abs_reciprocal_sqrt,
+                bias=eps[:, 0:1],
+                scale=1.0 / HIDDEN,
+            )
+            inv_std[i] = inverse
 
         def normalise(i):
             if not 0 <= i < N_TILES:
                 return
-            var_eps = stage.tile([P, 1], F32, tag="var_eps", bufs=3)
-            nc.gpsimd.tensor_scalar(
-                out=var_eps[:],
-                in0=squared[i][:],
-                scalar1=1.0 / HIDDEN,
-                scalar2=EPS,
-                op0=ALU.mult,
-                op1=ALU.add,
+            nc.vector.tensor_scalar(
+                out=normed[i][:],
+                in0=normed[i][:],
+                scalar1=minus_mean[i][:, 0:1],
+                scalar2=inv_std[i][:, 0:1],
+                op0=ALU.add,
+                op1=ALU.mult,
             )
-            inverse = stage.tile([P, 1], F32, tag="inv_std", bufs=3)
-            nc.gpsimd.tensor_tensor(out=inverse[:], in0=var_eps[:], in1=minus_half[:], op=ALU.pow)
-            for half in range(HALVES):
-                cols = slice(half * BANK, (half + 1) * BANK)
-                nc.gpsimd.tensor_scalar(
-                    out=normed[i][:, cols],
-                    in0=normed[i][:, cols],
-                    scalar1=minus_mean[i][:, 0:1],
-                    scalar2=inverse[:, 0:1],
-                    op0=ALU.add,
-                    op1=ALU.mult,
-                )
 
         def relu_slice(index):
             if not 0 <= index < N_GROUPS * SLICES:
@@ -352,7 +347,6 @@ def tile_sub_graph_pa_t_kernel(tc, x_nodes, w1, b1, gamma, beta, w2, b2, out):
             )
 
         transpose_x(0)
-        transpose_x(1)
 
         w1_codes = consts.tile([P, PASSES, HIDDEN], U32, align_bytes=64)
         w1_scales = consts.tile([P, PASSES, HIDDEN], U8, align_bytes=64)
@@ -391,16 +385,16 @@ def tile_sub_graph_pa_t_kernel(tc, x_nodes, w1, b1, gamma, beta, w2, b2, out):
             load_x(step + X_AHEAD)
             normalise(step - 2)
             regroup_r(due(step, QUANT_LAG, 2))
-            quantise_x(step + 1)
-            quantise_r(due(step, QUANT_LAG, 2))
-            transpose_x(step + 2)
+            transpose_x(step + 1)
             relu_slice(2 * (step - RELU_LAG))
             relu_slice(2 * (step - RELU_LAG) + 1)
             pool_pair(due(step, POOL_LAG, 2))
             store_pooled(due(step, STORE_LAG, GROUP))
             deviation(step - 1)
+            quantise_x(step + 1)
             first_layer(step)
             second_layer(due(step, LAYER2_LAG, 2))
+            quantise_r(due(step, QUANT_LAG, 2))
             if step == 0:
                 nc.vector.quantize_mx(
                     out=w2_codes[:].rearrange("p c n -> p (c n)").bitcast(FP8X4),

@@ -93,8 +93,8 @@ def tile_sub_graph_pa_t_kernel(tc, x_nodes, w1, b1, gamma, beta, w2, b2, out):
 
         affine_rows = consts.tile([P, P], BF16)
         nc.vector.memset(affine_rows[:], 0.0)
-        eps = consts.tile([P, 1], F32)
-        nc.vector.memset(eps[:], EPS)
+        minus_half = consts.tile([P, 1], F32)
+        nc.vector.memset(minus_half[:], -0.5)
         ident = consts.tile([P, P], F32)
         make_identity(nc, ident[:])
 
@@ -102,10 +102,12 @@ def tile_sub_graph_pa_t_kernel(tc, x_nodes, w1, b1, gamma, beta, w2, b2, out):
         nc.scalar.dma_start(
             out=affine_rows[SLICES : 2 * SLICES, :], in_=beta.rearrange("(s p) -> s p", p=P)
         )
-        b1_all = consts.tile([P, HIDDEN], BF16)
-        nc.scalar.dma_start(out=b1_all[:], in_=b1.partition_broadcast(P))
-        b2_all = consts.tile([P, FEATURES], BF16)
-        nc.scalar.dma_start(out=b2_all[:], in_=b2.partition_broadcast(P))
+        bias_rows = consts.tile([P, HIDDEN + FEATURES], BF16)
+        nc.vector.memset(bias_rows[:], 0.0)
+        ones = consts.tile([P, P], BF16)
+        nc.vector.memset(ones[:], 1.0)
+        nc.scalar.dma_start(out=bias_rows[0:1, 0:HIDDEN], in_=b1.rearrange("(o n) -> o n", o=1))
+        nc.scalar.dma_start(out=bias_rows[0:1, HIDDEN:], in_=b2.rearrange("(o n) -> o n", o=1))
 
         load_x(0)
         load_w1_half(0)
@@ -177,14 +179,14 @@ def tile_sub_graph_pa_t_kernel(tc, x_nodes, w1, b1, gamma, beta, w2, b2, out):
         def deviation(i):
             if not 0 <= i < N_TILES:
                 return
-            scaled_sums = stage.tile([P, HALVES], F32, tag="scaled_sums", bufs=2)
             negated = stage.tile([P, 1], F32, tag="minus_mean", bufs=6)
-            nc.scalar.activation(
-                out=scaled_sums[:],
-                in_=row_sums[i][:],
-                func=ACT.Identity,
-                scale=-1.0 / HIDDEN,
-                accum_out=negated[:, 0:1],
+            nc.gpsimd.tensor_scalar(
+                out=negated[:],
+                in0=row_sums[i][:, 0:1],
+                scalar1=row_sums[i][:, 1:2],
+                scalar2=-1.0 / HIDDEN,
+                op0=ALU.add,
+                op1=ALU.mult,
             )
             minus_mean[i] = negated
             squares = stage.tile([P, HIDDEN], BF16, tag="squares", bufs=2)
@@ -198,13 +200,16 @@ def tile_sub_graph_pa_t_kernel(tc, x_nodes, w1, b1, gamma, beta, w2, b2, out):
                 accum_out=sum_sq[:, 0:1],
             )
             inverse = stage.tile([P, 1], F32, tag="inv_std", bufs=4)
-            nc.scalar.activation(
-                out=inverse[:],
-                in_=sum_sq[:],
-                func=ACT.Abs_reciprocal_sqrt,
-                bias=eps[:, 0:1],
-                scale=1.0 / HIDDEN,
+            var_eps = stage.tile([P, 1], F32, tag="var_eps", bufs=3)
+            nc.gpsimd.tensor_scalar(
+                out=var_eps[:],
+                in0=sum_sq[:],
+                scalar1=1.0 / HIDDEN,
+                scalar2=EPS,
+                op0=ALU.mult,
+                op1=ALU.add,
             )
+            nc.gpsimd.tensor_tensor(out=inverse[:], in0=var_eps[:], in1=minus_half[:], op=ALU.pow)
             inv_std[i] = inverse
 
         def normalise(i):
@@ -288,7 +293,7 @@ def tile_sub_graph_pa_t_kernel(tc, x_nodes, w1, b1, gamma, beta, w2, b2, out):
             nc.vector.tensor_tensor(
                 out=x1_tiles[group][:, 2 * pair : 2 * pair + 2, :],
                 in0=x1_ps[:],
-                in1=b2_all[:].unsqueeze(1).to_broadcast([P, 2, FEATURES]),
+                in1=b2_all.unsqueeze(1).to_broadcast([P, 2, FEATURES]),
                 op=ALU.add,
             )
             if pair == GROUP // 2 - 1:
@@ -347,6 +352,21 @@ def tile_sub_graph_pa_t_kernel(tc, x_nodes, w1, b1, gamma, beta, w2, b2, out):
             )
 
         transpose_x(0)
+
+        bias_all = consts.tile([P, HIDDEN + FEATURES], BF16)
+        for first in range(0, HIDDEN + FEATURES, BANK):
+            width = min(BANK, HIDDEN + FEATURES - first)
+            bias_ps = psum.tile([P, BANK], F32, tag="h", bufs=2)
+            nc.tensor.matmul(
+                out=bias_ps[:, 0:width],
+                lhsT=ones[:],
+                rhs=bias_rows[:, first : first + width],
+                start=True,
+                stop=True,
+            )
+            nc.scalar.copy(out=bias_all[:, first : first + width], in_=bias_ps[:, 0:width])
+        b1_all = bias_all[:, 0:HIDDEN]
+        b2_all = bias_all[:, HIDDEN:]
 
         w1_codes = consts.tile([P, PASSES, HIDDEN], U32, align_bytes=64)
         w1_scales = consts.tile([P, PASSES, HIDDEN], U8, align_bytes=64)

@@ -44,6 +44,7 @@ LAYER2_LAG = 11
 POOL_LAG = LAYER2_LAG + 2
 STORE_LAG = POOL_LAG + 3
 N_STEPS = N_TILES - GROUP + STORE_LAG + 1
+SCALAR_SHARE = 4
 
 
 def due(step, lag, period):
@@ -93,8 +94,8 @@ def tile_sub_graph_pa_t_kernel(tc, x_nodes, w1, b1, gamma, beta, w2, b2, out):
 
         affine_rows = consts.tile([P, P], BF16)
         nc.vector.memset(affine_rows[:], 0.0)
-        minus_half = consts.tile([P, 1], F32)
-        nc.vector.memset(minus_half[:], -0.5)
+        eps = consts.tile([P, 1], F32)
+        nc.vector.memset(eps[:], EPS)
         ident = consts.tile([P, P], F32)
         make_identity(nc, ident[:])
 
@@ -179,14 +180,14 @@ def tile_sub_graph_pa_t_kernel(tc, x_nodes, w1, b1, gamma, beta, w2, b2, out):
         def deviation(i):
             if not 0 <= i < N_TILES:
                 return
+            scaled_sums = stage.tile([P, HALVES], F32, tag="scaled_sums", bufs=2)
             negated = stage.tile([P, 1], F32, tag="minus_mean", bufs=6)
-            nc.gpsimd.tensor_scalar(
-                out=negated[:],
-                in0=row_sums[i][:, 0:1],
-                scalar1=row_sums[i][:, 1:2],
-                scalar2=-1.0 / HIDDEN,
-                op0=ALU.add,
-                op1=ALU.mult,
+            nc.scalar.activation(
+                out=scaled_sums[:],
+                in_=row_sums[i][:],
+                func=ACT.Identity,
+                scale=-1.0 / HIDDEN,
+                accum_out=negated[:, 0:1],
             )
             minus_mean[i] = negated
             squares = stage.tile([P, HIDDEN], BF16, tag="squares", bufs=2)
@@ -200,20 +201,28 @@ def tile_sub_graph_pa_t_kernel(tc, x_nodes, w1, b1, gamma, beta, w2, b2, out):
                 accum_out=sum_sq[:, 0:1],
             )
             inverse = stage.tile([P, 1], F32, tag="inv_std", bufs=4)
-            var_eps = stage.tile([P, 1], F32, tag="var_eps", bufs=3)
-            nc.gpsimd.tensor_scalar(
-                out=var_eps[:],
-                in0=sum_sq[:],
-                scalar1=1.0 / HIDDEN,
-                scalar2=EPS,
-                op0=ALU.mult,
-                op1=ALU.add,
+            nc.scalar.activation(
+                out=inverse[:],
+                in_=sum_sq[:],
+                func=ACT.Abs_reciprocal_sqrt,
+                bias=eps[:, 0:1],
+                scale=1.0 / HIDDEN,
             )
-            nc.gpsimd.tensor_tensor(out=inverse[:], in0=var_eps[:], in1=minus_half[:], op=ALU.pow)
             inv_std[i] = inverse
 
         def normalise(i):
             if not 0 <= i < N_TILES:
+                return
+            if i % SCALAR_SHARE == 0:
+                shift = stage.tile([P, 1], F32, tag="shift", bufs=2)
+                nc.scalar.mul(out=shift[:], in_=minus_mean[i][:], mul=inv_std[i][:, 0:1])
+                nc.scalar.activation(
+                    out=normed[i][:],
+                    in_=normed[i][:],
+                    func=ACT.Identity,
+                    bias=shift[:, 0:1],
+                    scale=inv_std[i][:, 0:1],
+                )
                 return
             nc.vector.tensor_scalar(
                 out=normed[i][:],
@@ -326,7 +335,7 @@ def tile_sub_graph_pa_t_kernel(tc, x_nodes, w1, b1, gamma, beta, w2, b2, out):
             )
             if pair == GROUP // 2 - 1:
                 copies = stage.tile([P, FEATURES // P, GROUP_LINES, COPIES], F32, tag="repeated", bufs=2)
-                nc.vector.tensor_copy(
+                nc.scalar.copy(
                     out=copies[:],
                     in_=line_max[group][:].unsqueeze(3).to_broadcast([P, FEATURES // P, GROUP_LINES, COPIES]),
                 )
@@ -376,7 +385,9 @@ def tile_sub_graph_pa_t_kernel(tc, x_nodes, w1, b1, gamma, beta, w2, b2, out):
             grouped_passes = []
             for c in range(PASSES):
                 w1_grouped = stage.tile([P, BANK, PACK], BF16, tag="w1_grouped", bufs=2, align_bytes=64)
-                regroup(nc.vector.tensor_copy, w1_grouped[:], w1_planes[:, PACK * c : PACK * (c + 1), cols])
+                last = half == HALVES - 1 and c == PASSES - 1
+                copy = nc.scalar.copy if last else nc.vector.tensor_copy
+                regroup(copy, w1_grouped[:], w1_planes[:, PACK * c : PACK * (c + 1), cols])
                 grouped_passes.append(w1_grouped)
             for c in range(PASSES):
                 nc.vector.quantize_mx(

from contextlib import ExitStack

import concourse.mybir as mybir
from concourse.masks import make_identity

F32 = mybir.dt.float32
BF16 = mybir.dt.bfloat16
U32 = mybir.dt.uint32
U8 = mybir.dt.uint8
FP8X4 = mybir.dt.float8_e4m3fn_x4
ALU = mybir.AluOpType
ACT = mybir.ActivationFunctionType
AXIS = mybir.AxisListType

P = 128
PACK = 4
K_PASS = P * PACK
BANK = 512

TOKENS = 64 * 64
NODES = 64
HIDDEN = 1024
FEATURES = 256
PASSES = HIDDEN // K_PASS
SLICES = HIDDEN // P
GROUP = 4
GROUP_TOKENS = GROUP * P
N_GROUPS = TOKENS // GROUP_TOKENS
GROUP_LINES = GROUP_TOKENS // NODES
COPIES = P // GROUP_LINES
EPS = 1e-5

FLOPS = 2 * TOKENS * HIDDEN * (HIDDEN + FEATURES)


N_TILES = TOKENS // P
HALVES = HIDDEN // BANK
PAIR_LINES = 2 * P // NODES

X_AHEAD = 8
RELU_LAG = 6
QUANT_LAG = 8
LAYER2_LAG = 11
POOL_LAG = LAYER2_LAG + 2
STORE_LAG = POOL_LAG + 3
N_STEPS = N_TILES - GROUP + STORE_LAG + 1
SCALAR_SHARE = 4


def due(step, lag, period):
    if step < lag or (step - lag) % period != 0:
        return -1
    return (step - lag) // period


def regroup(copy, grouped, planes):
    copy(
        out=grouped.rearrange("p (n i) t -> p n t i", i=4),
        in_=planes.rearrange("p t (n i) -> p n t i", i=4),
    )


def tile_sub_graph_pa_t_kernel(tc, x_nodes, w1, b1, gamma, beta, w2, b2, out):
    nc = tc.nc
    x_rows = x_nodes.flatten_outer_dims()
    out_rows = out.flatten_outer_dims()

    with ExitStack() as ctx:
        consts = ctx.enter_context(tc.tile_pool(name="consts", bufs=1))
        stage = ctx.enter_context(tc.tile_pool(name="stage", bufs=2))
        psum = ctx.enter_context(tc.psum_pool(name="psum", bufs=1))

        x_tiles, x_words, x_quantised = {}, {}, {}
        normed, row_sums, minus_mean, inv_std = {}, {}, {}, {}
        r_planes, r_grouped, r_quantised = {}, {}, {}
        x1_tiles, line_max, repeated = {}, {}, {}

        def load_x(i):
            if i >= N_TILES:
                return
            x_sb = stage.tile([P, HIDDEN], BF16, tag="x_sb", bufs=X_AHEAD + 2)
            nc.sync.dma_start(out=x_sb[:], in_=x_rows[i * P : (i + 1) * P, :])
            x_tiles[i] = x_sb

        w1_planes = consts.tile([P, PASSES * PACK, HIDDEN], BF16)
        w1_quarters = w1.rearrange("(a q e) n -> a q e n", a=4, q=P, e=2)

        def load_w1_half(half):
            cols = slice(half * BANK, (half + 1) * BANK)
            for a in range(4):
                nc.sync.dma_start(
                    out=w1_planes[:, 2 * a : 2 * a + 2, cols], in_=w1_quarters[a][:, :, cols]
                )

        affine_rows = consts.tile([P, P], BF16)
        nc.vector.memset(affine_rows[:], 0.0)
        eps = consts.tile([P, 1], F32)
        nc.vector.memset(eps[:], EPS)
        ident = consts.tile([P, P], F32)
        make_identity(nc, ident[:])

        nc.scalar.dma_start(out=affine_rows[0:SLICES, :], in_=gamma.rearrange("(s p) -> s p", p=P))
        nc.scalar.dma_start(
            out=affine_rows[SLICES : 2 * SLICES, :], in_=beta.rearrange("(s p) -> s p", p=P)
        )
        bias_rows = consts.tile([P, HIDDEN + FEATURES], BF16)
        nc.vector.memset(bias_rows[:], 0.0)
        ones = consts.tile([P, P], BF16)
        nc.vector.memset(ones[:], 1.0)
        nc.scalar.dma_start(out=bias_rows[0:1, 0:HIDDEN], in_=b1.rearrange("(o n) -> o n", o=1))
        nc.scalar.dma_start(out=bias_rows[0:1, HIDDEN:], in_=b2.rearrange("(o n) -> o n", o=1))

        load_x(0)
        load_w1_half(0)
        load_x(1)
        load_w1_half(1)
        w2_planes = consts.tile([P, PASSES * PACK, FEATURES], BF16)
        nc.sync.dma_start(out=w2_planes[:], in_=w2.rearrange("(s p) n -> p s n", p=P))
        for i in range(2, X_AHEAD):
            load_x(i)

        def transpose_x(i):
            if i >= N_TILES:
                return
            words = x_tiles[i][:].bitcast(F32)
            xT_ps = psum.tile([P, PASSES, 2, P], F32, tag="xT", bufs=2)
            for c in range(PASSES):
                for u in range(2):
                    a = 2 * c + u
                    nc.tensor.transpose(
                        out=xT_ps[:, c, u, :], in_=words[:, a * P : (a + 1) * P], identity=ident[:]
                    )
            x_grouped = stage.tile([P, PASSES, P, 2], F32, tag="x_grouped", bufs=3, align_bytes=64)
            nc.scalar.copy(out=x_grouped[:], in_=xT_ps[:].rearrange("q c u r -> q c r u"))
            x_words[i] = x_grouped

        def quantise_x(i):
            if i >= N_TILES:
                return
            x_codes = stage.tile([P, PASSES, P], U32, tag="x_codes", bufs=3, align_bytes=64)
            x_scales = stage.tile([P, PASSES, P], U8, tag="x_scales", bufs=3, align_bytes=64)
            nc.vector.quantize_mx(
                out=x_codes[:].rearrange("q c r -> q (c r)").bitcast(FP8X4),
                scales=x_scales[:].rearrange("q c r -> q (c r)"),
                in_=x_words[i][:].rearrange("q c r u -> q (c r u)").bitcast(BF16),
            )
            x_quantised[i] = (x_codes, x_scales)

        def first_layer(i):
            if i >= N_TILES:
                return
            x_codes, x_scales = x_quantised[i]
            biased = stage.tile([P, HIDDEN], F32, tag="normed", bufs=12)
            sums = stage.tile([P, HALVES], F32, tag="sums", bufs=4)
            for half in range(HALVES):
                cols = slice(half * BANK, (half + 1) * BANK)
                h_ps = psum.tile([P, BANK], F32, tag="h", bufs=2)
                for c in range(PASSES):
                    nc.tensor.matmul_mx(
                        out=h_ps[:],
                        lhsT=x_codes[:, c, :].bitcast(FP8X4),
                        lhsT_scale=x_scales[:, c, :],
                        rhs=w1_codes[:, c, cols].bitcast(FP8X4),
                        rhs_scale=w1_scales[:, c, cols],
                        start=(c == 0),
                        stop=(c == PASSES - 1),
                    )
                nc.vector.scalar_tensor_tensor(
                    out=biased[:, cols],
                    in0=h_ps[:],
                    scalar=1.0,
                    in1=b1_all[:, cols],
                    op0=ALU.mult,
                    op1=ALU.add,
                    accum_out=sums[:, half : half + 1],
                )
            normed[i] = biased
            row_sums[i] = sums

        def deviation(i):
            if not 0 <= i < N_TILES:
                return
            scaled_sums = stage.tile([P, HALVES], F32, tag="scaled_sums", bufs=2)
            negated = stage.tile([P, 1], F32, tag="minus_mean", bufs=6)
            nc.scalar.activation(
                out=scaled_sums[:],
                in_=row_sums[i][:],
                func=ACT.Identity,
                scale=-1.0 / HIDDEN,
                accum_out=negated[:, 0:1],
            )
            minus_mean[i] = negated
            squares = stage.tile([P, HIDDEN], BF16, tag="squares", bufs=2)
            sum_sq = stage.tile([P, 1], F32, tag="sum_sq", bufs=3)
            nc.scalar.activation(
                out=squares[:],
                in_=normed[i][:],
                func=ACT.Square,
                bias=minus_mean[i][:, 0:1],
                scale=1.0,
                accum_out=sum_sq[:, 0:1],
            )
            inverse = stage.tile([P, 1], F32, tag="inv_std", bufs=4)
            nc.scalar.activation(
                out=inverse[:],
                in_=sum_sq[:],
                func=ACT.Abs_reciprocal_sqrt,
                bias=eps[:, 0:1],
                scale=1.0 / HIDDEN,
            )
            inv_std[i] = inverse

        def normalise(i):
            if not 0 <= i < N_TILES:
                return
            if i % SCALAR_SHARE == 0:
                shift = stage.tile([P, 1], F32, tag="shift", bufs=2)
                nc.scalar.mul(out=shift[:], in_=minus_mean[i][:], mul=inv_std[i][:, 0:1])
                nc.scalar.activation(
                    out=normed[i][:],
                    in_=normed[i][:],
                    func=ACT.Identity,
                    bias=shift[:, 0:1],
                    scale=inv_std[i][:, 0:1],
                )
                return
            nc.vector.tensor_scalar(
                out=normed[i][:],
                in0=normed[i][:],
                scalar1=minus_mean[i][:, 0:1],
                scalar2=inv_std[i][:, 0:1],
                op0=ALU.add,
                op1=ALU.mult,
            )

        def relu_slice(index):
            if not 0 <= index < N_GROUPS * SLICES:
                return
            group, s = divmod(index, SLICES)
            if s == 0:
                planes = stage.tile([P, SLICES, GROUP_TOKENS], BF16, tag="r_planes", bufs=2)
                r_planes[group] = planes
            normedT_ps = psum.tile([P, GROUP_TOKENS], F32, tag="normedT", bufs=2)
            for g in range(GROUP):
                nc.tensor.transpose(
                    out=normedT_ps[:, g * P : (g + 1) * P],
                    in_=normed[group * GROUP + g][:, s * P : (s + 1) * P],
                    identity=ident[:],
                )
            nc.scalar.activation(
                out=r_planes[group][:, s, :],
                in_=normedT_ps[:],
                func=ACT.Relu,
                bias=affine_cols[:, SLICES + s : SLICES + s + 1],
                scale=affine_cols[:, s : s + 1],
            )

        def regroup_r(index):
            if not 0 <= index < N_GROUPS * PASSES:
                return
            group, c = divmod(index, PASSES)
            grouped = stage.tile([P, GROUP_TOKENS, PACK], BF16, tag="r_grouped", bufs=2, align_bytes=64)
            regroup(nc.vector.tensor_copy, grouped[:], r_planes[group][:, PACK * c : PACK * (c + 1), :])
            r_grouped[index] = grouped

        def quantise_r(index):
            if not 0 <= index < N_GROUPS * PASSES:
                return
            group, c = divmod(index, PASSES)
            if c == 0:
                codes = stage.tile([P, PASSES, GROUP_TOKENS], U32, tag="r_codes", bufs=2, align_bytes=64)
                scales = stage.tile([P, PASSES, GROUP_TOKENS], U8, tag="r_scales", bufs=2, align_bytes=64)
                r_quantised[group] = (codes, scales)
            r_codes, r_scales = r_quantised[group]
            nc.vector.quantize_mx(
                out=r_codes[:, c, :].bitcast(FP8X4),
                scales=r_scales[:, c, :],
                in_=r_grouped[index][:].rearrange("p n t -> p (n t)"),
            )

        def second_layer(index):
            if not 0 <= index < N_TILES // 2:
                return
            group, pair = divmod(index, GROUP // 2)
            if pair == 0:
                x1_sb = stage.tile([P, GROUP, FEATURES], F32, tag="x1_sb", bufs=3)
                x1_tiles[group] = x1_sb
            r_codes, r_scales = r_quantised[group]
            x1_ps = psum.tile([P, 2, FEATURES], F32, tag="x1")
            for j in range(2):
                tokens = slice((2 * pair + j) * P, (2 * pair + j + 1) * P)
                for c in range(PASSES):
                    nc.tensor.matmul_mx(
                        out=x1_ps[:, j, :],
                        lhsT=r_codes[:, c, tokens].bitcast(FP8X4),
                        lhsT_scale=r_scales[:, c, tokens],
                        rhs=w2_codes[:, c, :].bitcast(FP8X4),
                        rhs_scale=w2_scales[:, c, :],
                        start=(c == 0),
                        stop=(c == PASSES - 1),
                    )
            nc.vector.tensor_tensor(
                out=x1_tiles[group][:, 2 * pair : 2 * pair + 2, :],
                in0=x1_ps[:],
                in1=b2_all.unsqueeze(1).to_broadcast([P, 2, FEATURES]),
                op=ALU.add,
            )
            if pair == GROUP // 2 - 1:
                rows = slice(group * GROUP_TOKENS, (group + 1) * GROUP_TOKENS)
                nc.sync.dma_start(
                    out=out_rows[rows, 0:FEATURES].rearrange("(g p) f -> p g f", p=P),
                    in_=x1_tiles[group][:],
                )

        def pool_pair(index):
            if not 0 <= index < N_TILES // 2:
                return
            group, pair = divmod(index, GROUP // 2)
            if pair == 0:
                maxima = stage.tile([P, FEATURES // P, GROUP_LINES], F32, tag="line_max", bufs=2)
                line_max[group] = maxima
            x1T_ps = psum.tile([P, FEATURES // P, 2 * P], F32, tag="pooled")
            for s in range(FEATURES // P):
                for j in range(2):
                    nc.tensor.transpose(
                        out=x1T_ps[:, s, j * P : (j + 1) * P],
                        in_=x1_tiles[group][:, 2 * pair + j, s * P : (s + 1) * P],
                        identity=ident[:],
                    )
            nc.vector.tensor_reduce(
                out=line_max[group][:, :, pair * PAIR_LINES : (pair + 1) * PAIR_LINES],
                in_=x1T_ps[:].rearrange("f s (b l) -> f s b l", l=NODES),
                axis=AXIS.X,
                op=ALU.max,
            )
            if pair == GROUP // 2 - 1:
                copies = stage.tile([P, FEATURES // P, GROUP_LINES, COPIES], F32, tag="repeated", bufs=2)
                nc.scalar.copy(
                    out=copies[:],
                    in_=line_max[group][:].unsqueeze(3).to_broadcast([P, FEATURES // P, GROUP_LINES, COPIES]),
                )
                repeated[group] = copies

        def store_pooled(group):
            if not 0 <= group < N_GROUPS:
                return
            x2_ps = psum.tile([P, FEATURES], F32, tag="pooled")
            for s in range(FEATURES // P):
                nc.tensor.transpose(
                    out=x2_ps[:, s * P : (s + 1) * P],
                    in_=repeated[group][:, s, :, :].rearrange("f b i -> f (b i)"),
                    identity=ident[:],
                )
            x2_sb = stage.tile([P, FEATURES], F32, tag="x2_sb", bufs=2)
            nc.scalar.copy(out=x2_sb[:], in_=x2_ps[:])
            rows = slice(group * GROUP_TOKENS, (group + 1) * GROUP_TOKENS)
            nodes_each = NODES // COPIES
            nc.sync.dma_start(
                out=out_rows[rows, FEATURES : 2 * FEATURES].rearrange("(p m) f -> p m f", m=nodes_each),
                in_=x2_sb[:].unsqueeze(1).to_broadcast([P, nodes_each, FEATURES]),
            )

        transpose_x(0)

        bias_all = consts.tile([P, HIDDEN + FEATURES], BF16)
        for first in range(0, HIDDEN + FEATURES, BANK):
            width = min(BANK, HIDDEN + FEATURES - first)
            bias_ps = psum.tile([P, BANK], F32, tag="h", bufs=2)
            nc.tensor.matmul(
                out=bias_ps[:, 0:width],
                lhsT=ones[:],
                rhs=bias_rows[:, first : first + width],
                start=True,
                stop=True,
            )
            nc.scalar.copy(out=bias_all[:, first : first + width], in_=bias_ps[:, 0:width])
        b1_all = bias_all[:, 0:HIDDEN]
        b2_all = bias_all[:, HIDDEN:]

        w1_codes = consts.tile([P, PASSES, HIDDEN], U32, align_bytes=64)
        w1_scales = consts.tile([P, PASSES, HIDDEN], U8, align_bytes=64)

        def quantise_w1_half(half):
            cols = slice(half * BANK, (half + 1) * BANK)
            grouped_passes = []
            for c in range(PASSES):
                w1_grouped = stage.tile([P, BANK, PACK], BF16, tag="w1_grouped", bufs=2, align_bytes=64)
                last = half == HALVES - 1 and c == PASSES - 1
                copy = nc.scalar.copy if last else nc.vector.tensor_copy
                regroup(copy, w1_grouped[:], w1_planes[:, PACK * c : PACK * (c + 1), cols])
                grouped_passes.append(w1_grouped)
            for c in range(PASSES):
                nc.vector.quantize_mx(
                    out=w1_codes[:, c, cols].bitcast(FP8X4),
                    scales=w1_scales[:, c, cols],
                    in_=grouped_passes[c][:].rearrange("p n t -> p (n t)"),
                )

        quantise_w1_half(0)
        quantise_x(0)
        affine_f32 = consts.tile([P, P], F32)
        nc.vector.tensor_copy(out=affine_f32[:], in_=affine_rows[:])
        affine_ps = psum.tile([P, P], F32, tag="pooled")
        nc.tensor.transpose(out=affine_ps[:], in_=affine_f32[:], identity=ident[:])
        quantise_w1_half(1)
        affine_cols = consts.tile([P, 2 * SLICES], F32)
        nc.vector.tensor_copy(out=affine_cols[:], in_=affine_ps[:, 0 : 2 * SLICES])

        w2_grouped = consts.tile([P, PASSES, FEATURES, PACK], BF16, align_bytes=64)
        for c in range(PASSES):
            regroup(nc.scalar.copy, w2_grouped[:, c, :, :], w2_planes[:, PACK * c : PACK * (c + 1), :])
        w2_codes = consts.tile([P, PASSES, FEATURES], U32, align_bytes=64)
        w2_scales = consts.tile([P, PASSES, FEATURES], U8, align_bytes=64)

        for step in range(N_STEPS):
            load_x(step + X_AHEAD)
            normalise(step - 2)
            regroup_r(due(step, QUANT_LAG, 2))
            transpose_x(step + 1)
            relu_slice(2 * (step - RELU_LAG))
            relu_slice(2 * (step - RELU_LAG) + 1)
            pool_pair(due(step, POOL_LAG, 2))
            store_pooled(due(step, STORE_LAG, GROUP))
            deviation(step - 1)
            quantise_x(step + 1)
            first_layer(step)
            second_layer(due(step, LAYER2_LAG, 2))
            quantise_r(due(step, QUANT_LAG, 2))
            if step == 0:
                nc.vector.quantize_mx(
                    out=w2_codes[:].rearrange("p c n -> p (c n)").bitcast(FP8X4),
                    scales=w2_scales[:].rearrange("p c n -> p (c n)"),
                    in_=w2_grouped[:].rearrange("p c n t -> p (c n t)"),
                )
